import numpy as np
import ml_dtypes

BF16 = ml_dtypes.bfloat16


def bf(x):
    return np.asarray(x, np.float32).astype(BF16)


def f32(x):
    return np.asarray(x, np.float32)


def f64(x):
    return np.asarray(x).astype(np.float64)


def striped(idx):
    return np.tile(idx.reshape(-1, 16).T, (8, 1))


C, S, K, H, N = 256, 256, 2, 128, 256


def setup_inputs():
    raw = np.random.standard_normal((C, S))
    x = f32(raw * np.sqrt(C) / np.sqrt((raw * raw).sum(axis=0, keepdims=True)))
    o = bf(np.random.standard_normal((C, N)))
    w = bf(np.random.standard_normal((K, C, C)) / np.sqrt(C))
    idx = np.concatenate([np.random.permutation(S)[:H] for _ in range(K)])
    return {"x": x, "o": o, "w": w, "offs": striped(idx)}


def reference(x, o, w, offs):
    idx = offs[:16].T.reshape(-1)
    t = np.concatenate([f64(w)[r].T @ f64(o)[:, r * H:(r + 1) * H] for r in range(K)], axis=1)
    return f64(x)[:, idx] * t

@@ -1,0 +1,50 @@
+import concourse.mybir as mybir
+
+P = 128
+C, K, H, N = 256, 2, 128, 256
+S = 256
+BLOCKS = C // P
+FLOPS = 2 * C * C * N
+
+BF16, F32, U16 = mybir.dt.bfloat16, mybir.dt.float32, mybir.dt.uint16
+MULT = mybir.AluOpType.mult
+COPY = mybir.ActivationFunctionType.Copy
+
+
+def tile_rescal_kernel(tc, x, o, w, offs, out):
+    nc = tc.nc
+    with (
+        tc.tile_pool(name="held", bufs=1) as held,
+        tc.tile_pool(name="work", bufs=K * BLOCKS) as work,
+        tc.psum_pool(name="psum", bufs=K * BLOCKS) as psum,
+    ):
+        o_sb = held.tile([P, BLOCKS, N], BF16, name="o_sb")
+        w_sb = held.tile([P, K, BLOCKS, C], BF16, name="w_sb")
+        offsets = held.tile([P, N // 16], U16, name="offsets")
+        x_sb = [held.tile([P, S], F32, name=f"x_sb{cb}") for cb in range(BLOCKS)]
+
+        nc.sync.dma_start(w_sb[:, 0], w[0].rearrange("(p b) c -> p b c", b=BLOCKS))
+        nc.scalar.dma_start(o_sb[:], o.rearrange("(p b) j -> p b j", b=BLOCKS))
+        nc.scalar.dma_start(w_sb[:, 1], w[1].rearrange("(p b) c -> p b c", b=BLOCKS))
+        nc.sync.dma_start(offsets[:], offs)
+        nc.sync.dma_start(x_sb[0][:], x[0:P, :])
+        nc.scalar.dma_start(x_sb[1][:], x[P:2 * P, :])
+
+        store_queues = (nc.scalar, nc.sync)
+        out_blocks = out.rearrange("(cb p) j -> p cb j", p=P)
+        for r in range(K):
+            edges = slice(r * H, (r + 1) * H)
+            prod = held.tile([P, BLOCKS, H], F32, name=f"prod{r}")
+            for cb in range(BLOCKS):
+                channels = slice(cb * P, (cb + 1) * P)
+                t_ps = psum.tile([P, H], F32, name="t_ps")
+                for b in range(BLOCKS):
+                    nc.tensor.matmul(
+                        t_ps[:], w_sb[:, r, b, channels], o_sb[:, b, edges],
+                        start=(b == 0), stop=(b == BLOCKS - 1),
+                    )
+                t_sb = work.tile([P, H], F32, name="t_sb")
+                nc.scalar.activation(t_sb[:], t_ps[:], COPY)
+                picked = x_sb[cb][:].indirect(offsets[:, r * H // 16:(r + 1) * H // 16])
+                nc.vector.tensor_tensor(prod[:, cb, :], picked, t_sb[:], MULT)
+            store_queues[r].dma_start(out_blocks[:, :, edges], prod[:])

@@ -8,7 +8,6 @@ FLOPS = 2 * C * C * N
 
 BF16, F32, U16 = mybir.dt.bfloat16, mybir.dt.float32, mybir.dt.uint16
 MULT = mybir.AluOpType.mult
-COPY = mybir.ActivationFunctionType.Copy
 
 
 def tile_rescal_kernel(tc, x, o, w, offs, out):
@@ -44,7 +43,7 @@ def tile_rescal_kernel(tc, x, o, w, offs, out):
                         start=(b == 0), stop=(b == BLOCKS - 1),
                     )
                 t_sb = work.tile([P, H], F32, name="t_sb")
-                nc.scalar.activation(t_sb[:], t_ps[:], COPY)
+                nc.scalar.copy(t_sb[:], t_ps[:])
                 picked = x_sb[cb][:].indirect(offsets[:, r * H // 16:(r + 1) * H // 16])
                 nc.vector.tensor_tensor(prod[:, cb, :], picked, t_sb[:], MULT)
             store_queues[r].dma_start(out_blocks[:, :, edges], prod[:])

@@ -23,13 +23,13 @@ def tile_rescal_kernel(tc, x, o, w, offs, out):
         x_sb = [held.tile([P, S], F32, name=f"x_sb{cb}") for cb in range(BLOCKS)]
 
         nc.sync.dma_start(w_sb[:, 0], w[0].rearrange("(p b) c -> p b c", b=BLOCKS))
-        nc.scalar.dma_start(o_sb[:], o.rearrange("(p b) j -> p b j", b=BLOCKS))
-        nc.scalar.dma_start(w_sb[:, 1], w[1].rearrange("(p b) c -> p b c", b=BLOCKS))
+        nc.sync.dma_start(o_sb[:], o.rearrange("(p b) j -> p b j", b=BLOCKS))
+        nc.sync.dma_start(w_sb[:, 1], w[1].rearrange("(p b) c -> p b c", b=BLOCKS))
         nc.sync.dma_start(offsets[:], offs)
         nc.sync.dma_start(x_sb[0][:], x[0:P, :])
-        nc.scalar.dma_start(x_sb[1][:], x[P:2 * P, :])
+        nc.sync.dma_start(x_sb[1][:], x[P:2 * P, :])
 
-        store_queues = (nc.scalar, nc.sync)
+        store_queues = (nc.sync, nc.sync)
         out_blocks = out.rearrange("(cb p) j -> p cb j", p=P)
         for r in range(K):
             edges = slice(r * H, (r + 1) * H)

@@ -14,8 +14,8 @@ def tile_rescal_kernel(tc, x, o, w, offs, out):
     nc = tc.nc
     with (
         tc.tile_pool(name="held", bufs=1) as held,
-        tc.tile_pool(name="work", bufs=K * BLOCKS) as work,
-        tc.psum_pool(name="psum", bufs=K * BLOCKS) as psum,
+        tc.tile_pool(name="work", bufs=K * BLOCKS + 1) as work,
+        tc.psum_pool(name="psum", bufs=K * BLOCKS + 1) as psum,
     ):
         o_sb = held.tile([P, BLOCKS, N], BF16, name="o_sb")
         w_sb = held.tile([P, K, BLOCKS, C], BF16, name="w_sb")
@@ -36,14 +36,21 @@ def tile_rescal_kernel(tc, x, o, w, offs, out):
             prod = held.tile([P, BLOCKS, H], F32, name=f"prod{r}")
             for cb in range(BLOCKS):
                 channels = slice(cb * P, (cb + 1) * P)
-                t_ps = psum.tile([P, H], F32, name="t_ps")
-                for b in range(BLOCKS):
-                    nc.tensor.matmul(
-                        t_ps[:], w_sb[:, r, b, channels], o_sb[:, b, edges],
-                        start=(b == 0), stop=(b == BLOCKS - 1),
-                    )
-                t_sb = work.tile([P, H], F32, name="t_sb")
-                nc.scalar.copy(t_sb[:], t_ps[:])
-                picked = x_sb[cb][:].indirect(offsets[:, r * H // 16:(r + 1) * H // 16])
-                nc.vector.tensor_tensor(prod[:, cb, :], picked, t_sb[:], MULT)
+                parts = 2 if r == 0 and cb == 0 else 1
+                n = H // parts
+                for part in range(parts):
+                    first = r * H + part * n
+                    t_ps = psum.tile([P, n], F32, name="t_ps")
+                    for b in range(BLOCKS):
+                        nc.tensor.matmul(
+                            t_ps[:], w_sb[:, r, b, channels], o_sb[:, b, first:first + n],
+                            start=(b == 0), stop=(b == BLOCKS - 1),
+                        )
+                    t_sb = work.tile([P, n], F32, name="t_sb")
+                    if parts == 2 and part == 0:
+                        nc.vector.tensor_copy(t_sb[:], t_ps[:])
+                    else:
+                        nc.scalar.copy(t_sb[:], t_ps[:])
+                    picked = x_sb[cb][:].indirect(offsets[:, first // 16:(first + n) // 16])
+                    nc.vector.tensor_tensor(prod[:, cb, part * n:(part + 1) * n], picked, t_sb[:], MULT)
             store_queues[r].dma_start(out_blocks[:, :, edges], prod[:])

import concourse.mybir as mybir

P = 128
C, K, H, N = 256, 2, 128, 256
S = 256
BLOCKS = C // P
FLOPS = 2 * C * C * N

BF16, F32, U16 = mybir.dt.bfloat16, mybir.dt.float32, mybir.dt.uint16
MULT = mybir.AluOpType.mult


def tile_rescal_kernel(tc, x, o, w, offs, out):
    nc = tc.nc
    with (
        tc.tile_pool(name="held", bufs=1) as held,
        tc.tile_pool(name="work", bufs=K * BLOCKS + 1) as work,
        tc.psum_pool(name="psum", bufs=K * BLOCKS + 1) as psum,
    ):
        o_sb = held.tile([P, BLOCKS, N], BF16, name="o_sb")
        w_sb = held.tile([P, K, BLOCKS, C], BF16, name="w_sb")
        offsets = held.tile([P, N // 16], U16, name="offsets")
        x_sb = [held.tile([P, S], F32, name=f"x_sb{cb}") for cb in range(BLOCKS)]

        nc.sync.dma_start(w_sb[:, 0], w[0].rearrange("(p b) c -> p b c", b=BLOCKS))
        nc.sync.dma_start(o_sb[:], o.rearrange("(p b) j -> p b j", b=BLOCKS))
        nc.sync.dma_start(w_sb[:, 1], w[1].rearrange("(p b) c -> p b c", b=BLOCKS))
        nc.sync.dma_start(offsets[:], offs)
        nc.sync.dma_start(x_sb[0][:], x[0:P, :])
        nc.sync.dma_start(x_sb[1][:], x[P:2 * P, :])

        store_queues = (nc.sync, nc.sync)
        out_blocks = out.rearrange("(cb p) j -> p cb j", p=P)
        for r in range(K):
            edges = slice(r * H, (r + 1) * H)
            prod = held.tile([P, BLOCKS, H], F32, name=f"prod{r}")
            for cb in range(BLOCKS):
                channels = slice(cb * P, (cb + 1) * P)
                parts = 2 if r == 0 and cb == 0 else 1
                n = H // parts
                for part in range(parts):
                    first = r * H + part * n
                    t_ps = psum.tile([P, n], F32, name="t_ps")
                    for b in range(BLOCKS):
                        nc.tensor.matmul(
                            t_ps[:], w_sb[:, r, b, channels], o_sb[:, b, first:first + n],
                            start=(b == 0), stop=(b == BLOCKS - 1),
                        )
                    t_sb = work.tile([P, n], F32, name="t_sb")
                    if parts == 2 and part == 0:
                        nc.vector.tensor_copy(t_sb[:], t_ps[:])
                    else:
                        nc.scalar.copy(t_sb[:], t_ps[:])
                    picked = x_sb[cb][:].indirect(offsets[:, first // 16:(first + n) // 16])
                    nc.vector.tensor_tensor(prod[:, cb, part * n:(part + 1) * n], picked, t_sb[:], MULT)
            store_queues[r].dma_start(out_blocks[:, :, edges], prod[:])
